import numpy as np
import ml_dtypes

BF16 = ml_dtypes.bfloat16


def bf(x):
    return np.asarray(x, np.float32).astype(BF16)


def f32(x):
    return np.asarray(x, np.float32)


def f64(x):
    return np.asarray(x).astype(np.float64)


def striped(idx):
    return np.tile(idx.reshape(-1, 16).T, (8, 1))


V, D, M, N = 1024, 128, 512, 256
PE_BASE = 10000.0


def sinusoidal_pe():
    pos = np.arange(N, dtype=np.float32)[None, :]
    i = np.arange(D, dtype=np.float32)[:, None]
    ang = pos / np.power(np.float32(PE_BASE), i / np.float32(D))
    return np.where(np.arange(D)[:, None] % 2 == 0, np.sin(ang), np.cos(ang))


def setup_inputs():
    return {"table": bf(np.random.standard_normal((V, D))), "w": bf(np.random.standard_normal((D, M)) / np.sqrt(D)), "b": f32(0.1 * np.random.standard_normal((M, 1))), "pe": f32(sinusoidal_pe()), "offs": striped(np.random.permutation(np.tile(np.arange(V), 2))[:N])}


def reference(table, w, b, pe, offs):
    idx = offs[:16].T.reshape(-1)
    return f64(w).T @ (f64(table)[idx].T + f64(pe)) + f64(b)

@@ -1,0 +1,74 @@
+import concourse.mybir as mybir
+from concourse.masks import make_identity
+
+BF16, F32, U16 = mybir.dt.bfloat16, mybir.dt.float32, mybir.dt.uint16
+
+P = 128
+V, D, M, N = 1024, 128, 512, 256
+BLOCKS = V // P
+CHUNKS = 4
+BLOCKS_PER_CHUNK = BLOCKS // CHUNKS
+C = M // P
+
+FLOPS = 2 * (2 * D * M * N)
+
+
+def tile_fullencoder_kernel(tc, table, w, b, pe, offs, out):
+    nc = tc.nc
+    with (
+        tc.tile_pool(name="held", bufs=1) as held,
+        tc.psum_pool(name="flip", bufs=1) as flip,
+        tc.psum_pool(name="sums", bufs=1) as sums,
+    ):
+        identity = held.tile([P, P], BF16, name="identity")
+        make_identity(nc, identity[:])
+
+        offsets = held.tile([P, N // 16], U16, name="offsets")
+        nc.sync.dma_start(offsets[:], offs)
+
+        table_blocks = table.rearrange("(t p) k -> p t k", p=P)
+        words = []
+        for q in range(CHUNKS):
+            chunk = held.tile([P, BLOCKS_PER_CHUNK, D], BF16, name=f"words{q}")
+            queue = nc.sync if q % 2 == 0 else nc.scalar
+            queue.dma_start(chunk[:], table_blocks[:, q * BLOCKS_PER_CHUNK : (q + 1) * BLOCKS_PER_CHUNK, :])
+            words.append(chunk)
+
+        w_sb = held.tile([D, M], BF16, name="w_sb")
+        nc.sync.dma_start(w_sb[:], w)
+        pe_f32 = held.tile([D, N], F32, name="pe_f32")
+        nc.scalar.dma_start(pe_f32[:], pe)
+        bias = held.tile([P, C], F32, name="bias")
+        nc.scalar.dma_start(bias[:], b.rearrange("(p c) o -> p (c o)", c=C))
+
+        pe_bf = held.tile([D, N], BF16, name="pe_bf")
+        nc.vector.tensor_copy(pe_bf[:], pe_f32[:])
+        w_cols = held.tile([D, C, P], BF16, name="w_cols")
+        nc.gpsimd.tensor_copy(w_cols[:], w_sb[:].rearrange("k (p c) -> k c p", c=C))
+        acc = [sums.tile([P, N], F32, name=f"acc{c}") for c in range(C)]
+        for c in range(C):
+            nc.tensor.matmul(acc[c][:], w_cols[:, c, :], pe_bf[:], start=True, stop=False)
+
+        window = held.tile([D, V], BF16, name="window")
+        for q in range(CHUNKS):
+            flipped = flip.tile([D, BLOCKS_PER_CHUNK * P], BF16, name=f"flipped{q}")
+            for t in range(BLOCKS_PER_CHUNK):
+                nc.tensor.transpose(flipped[:, t * P : (t + 1) * P], words[q][:, t, :], identity[:])
+            columns = window[:, q * BLOCKS_PER_CHUNK * P : (q + 1) * BLOCKS_PER_CHUNK * P]
+            if q % 2 == 0:
+                nc.vector.tensor_copy(columns, flipped[:])
+            else:
+                nc.scalar.copy(columns, flipped[:])
+
+        out_rows = out.rearrange("(p c) j -> p c j", c=C)
+        for c in range(C):
+            nc.tensor.matmul(acc[c][:], w_cols[:, c, :], window[:].indirect(offsets[:]), start=False, stop=True)
+            result = held.tile([P, N], F32, name=f"result{c}")
+            if c % 2 == 0:
+                nc.vector.tensor_scalar(result[:], acc[c][:], bias[:, c : c + 1], None, mybir.AluOpType.add)
+                nc.sync.dma_start(out_rows[:, c, :], result[:])
+            else:
+                nc.scalar.activation(
+                    result[:], acc[c][:], mybir.ActivationFunctionType.Identity, bias=bias[:, c : c + 1]
+                )
+                nc.scalar.dma_start(out_rows[:, c, :], result[:])

@@ -23,9 +23,6 @@ def tile_fullencoder_kernel(tc, table, w, b, pe, offs, out):
         identity = held.tile([P, P], BF16, name="identity")
         make_identity(nc, identity[:])
 
-        offsets = held.tile([P, N // 16], U16, name="offsets")
-        nc.sync.dma_start(offsets[:], offs)
-
         table_blocks = table.rearrange("(t p) k -> p t k", p=P)
         words = []
         for q in range(CHUNKS):
@@ -33,21 +30,14 @@ def tile_fullencoder_kernel(tc, table, w, b, pe, offs, out):
             queue = nc.sync if q % 2 == 0 else nc.scalar
             queue.dma_start(chunk[:], table_blocks[:, q * BLOCKS_PER_CHUNK : (q + 1) * BLOCKS_PER_CHUNK, :])
             words.append(chunk)
-
         w_sb = held.tile([D, M], BF16, name="w_sb")
         nc.sync.dma_start(w_sb[:], w)
         pe_f32 = held.tile([D, N], F32, name="pe_f32")
         nc.scalar.dma_start(pe_f32[:], pe)
+        offsets = held.tile([P, N // 16], U16, name="offsets")
+        nc.sync.dma_start(offsets[:], offs)
         bias = held.tile([P, C], F32, name="bias")
         nc.scalar.dma_start(bias[:], b.rearrange("(p c) o -> p (c o)", c=C))
-
-        pe_bf = held.tile([D, N], BF16, name="pe_bf")
-        nc.vector.tensor_copy(pe_bf[:], pe_f32[:])
-        w_cols = held.tile([D, C, P], BF16, name="w_cols")
-        nc.gpsimd.tensor_copy(w_cols[:], w_sb[:].rearrange("k (p c) -> k c p", c=C))
-        acc = [sums.tile([P, N], F32, name=f"acc{c}") for c in range(C)]
-        for c in range(C):
-            nc.tensor.matmul(acc[c][:], w_cols[:, c, :], pe_bf[:], start=True, stop=False)
 
         window = held.tile([D, V], BF16, name="window")
         for q in range(CHUNKS):
@@ -59,6 +49,14 @@ def tile_fullencoder_kernel(tc, table, w, b, pe, offs, out):
                 nc.vector.tensor_copy(columns, flipped[:])
             else:
                 nc.scalar.copy(columns, flipped[:])
+
+        w_cols = held.tile([D, C, P], BF16, name="w_cols")
+        nc.vector.tensor_copy(w_cols[:], w_sb[:].rearrange("k (p c) -> k c p", c=C))
+        pe_bf = held.tile([D, N], BF16, name="pe_bf")
+        nc.gpsimd.tensor_copy(pe_bf[:], pe_f32[:])
+        acc = [sums.tile([P, N], F32, name=f"acc{c}") for c in range(C)]
+        for c in range(C):
+            nc.tensor.matmul(acc[c][:], w_cols[:, c, :], pe_bf[:], start=True, stop=False)
 
         out_rows = out.rearrange("(p c) j -> p c j", c=C)
         for c in range(C):

@@ -37,7 +37,8 @@ def tile_fullencoder_kernel(tc, table, w, b, pe, offs, out):
         offsets = held.tile([P, N // 16], U16, name="offsets")
         nc.sync.dma_start(offsets[:], offs)
         bias = held.tile([P, C], F32, name="bias")
-        nc.scalar.dma_start(bias[:], b.rearrange("(p c) o -> p (c o)", c=C))
+        with nc.allow_non_contiguous_dma(reason="512 biases, four to a partition, 128 apart in HBM"):
+            nc.scalar.dma_start(bias[:], b.rearrange("(c p) o -> p (c o)", p=P))
 
         window = held.tile([D, V], BF16, name="window")
         for q in range(CHUNKS):
@@ -50,17 +51,15 @@ def tile_fullencoder_kernel(tc, table, w, b, pe, offs, out):
             else:
                 nc.scalar.copy(columns, flipped[:])
 
-        w_cols = held.tile([D, C, P], BF16, name="w_cols")
-        nc.vector.tensor_copy(w_cols[:], w_sb[:].rearrange("k (p c) -> k c p", c=C))
         pe_bf = held.tile([D, N], BF16, name="pe_bf")
         nc.gpsimd.tensor_copy(pe_bf[:], pe_f32[:])
         acc = [sums.tile([P, N], F32, name=f"acc{c}") for c in range(C)]
         for c in range(C):
-            nc.tensor.matmul(acc[c][:], w_cols[:, c, :], pe_bf[:], start=True, stop=False)
+            nc.tensor.matmul(acc[c][:], w_sb[:, c * P : (c + 1) * P], pe_bf[:], start=True, stop=False)
 
-        out_rows = out.rearrange("(p c) j -> p c j", c=C)
+        out_rows = out.rearrange("(c p) j -> p c j", p=P)
         for c in range(C):
-            nc.tensor.matmul(acc[c][:], w_cols[:, c, :], window[:].indirect(offsets[:]), start=False, stop=True)
+            nc.tensor.matmul(acc[c][:], w_sb[:, c * P : (c + 1) * P], window[:].indirect(offsets[:]), start=False, stop=True)
             result = held.tile([P, N], F32, name=f"result{c}")
             if c % 2 == 0:
                 nc.vector.tensor_scalar(result[:], acc[c][:], bias[:, c : c + 1], None, mybir.AluOpType.add)

@@ -9,6 +9,7 @@ BLOCKS = V // P
 CHUNKS = 4
 BLOCKS_PER_CHUNK = BLOCKS // CHUNKS
 C = M // P
+WARMERS = 6
 
 FLOPS = 2 * (2 * D * M * N)
 
@@ -20,6 +21,12 @@ def tile_fullencoder_kernel(tc, table, w, b, pe, offs, out):
         tc.psum_pool(name="flip", bufs=1) as flip,
         tc.psum_pool(name="sums", bufs=1) as sums,
     ):
+        zeros = held.tile([P, N], BF16, name="zeros")
+        nc.gpsimd.memset(zeros[:], 0.0)
+        acc = [sums.tile([P, N], F32, name=f"acc{c}") for c in range(C)]
+        for warmer in range(WARMERS):
+            nc.tensor.matmul(acc[warmer % C][:], zeros[:, 0:P], zeros[:], start=True, stop=True)
+
         identity = held.tile([P, P], BF16, name="identity")
         make_identity(nc, identity[:])
 
@@ -53,7 +60,6 @@ def tile_fullencoder_kernel(tc, table, w, b, pe, offs, out):
 
         pe_bf = held.tile([D, N], BF16, name="pe_bf")
         nc.gpsimd.tensor_copy(pe_bf[:], pe_f32[:])
-        acc = [sums.tile([P, N], F32, name=f"acc{c}") for c in range(C)]
         for c in range(C):
             nc.tensor.matmul(acc[c][:], w_sb[:, c * P : (c + 1) * P], pe_bf[:], start=True, stop=False)
 

@@ -58,14 +58,14 @@ def tile_fullencoder_kernel(tc, table, w, b, pe, offs, out):
             else:
                 nc.scalar.copy(columns, flipped[:])
 
+        for c in range(C):
+            nc.tensor.matmul(acc[c][:], w_sb[:, c * P : (c + 1) * P], window[:].indirect(offsets[:]), start=True, stop=False)
+
         pe_bf = held.tile([D, N], BF16, name="pe_bf")
         nc.gpsimd.tensor_copy(pe_bf[:], pe_f32[:])
-        for c in range(C):
-            nc.tensor.matmul(acc[c][:], w_sb[:, c * P : (c + 1) * P], pe_bf[:], start=True, stop=False)
-
         out_rows = out.rearrange("(c p) j -> p c j", p=P)
         for c in range(C):
-            nc.tensor.matmul(acc[c][:], w_sb[:, c * P : (c + 1) * P], window[:].indirect(offsets[:]), start=False, stop=True)
+            nc.tensor.matmul(acc[c][:], w_sb[:, c * P : (c + 1) * P], pe_bf[:], start=False, stop=True)
             result = held.tile([P, N], F32, name=f"result{c}")
             if c % 2 == 0:
                 nc.vector.tensor_scalar(result[:], acc[c][:], bias[:, c : c + 1], None, mybir.AluOpType.add)

@@ -30,33 +30,35 @@ def tile_fullencoder_kernel(tc, table, w, b, pe, offs, out):
         identity = held.tile([P, P], BF16, name="identity")
         make_identity(nc, identity[:])
 
-        table_blocks = table.rearrange("(t p) k -> p t k", p=P)
+        offsets = held.tile([P, N // 16], U16, name="offsets")
+        nc.sync.dma_start(offsets[:], offs)
+        table_chunks = table.rearrange("(q p t) k -> p q t k", p=P, t=BLOCKS_PER_CHUNK)
         words = []
         for q in range(CHUNKS):
             chunk = held.tile([P, BLOCKS_PER_CHUNK, D], BF16, name=f"words{q}")
             queue = nc.sync if q % 2 == 0 else nc.scalar
-            queue.dma_start(chunk[:], table_blocks[:, q * BLOCKS_PER_CHUNK : (q + 1) * BLOCKS_PER_CHUNK, :])
+            queue.dma_start(chunk[:], table_chunks[:, q, :, :])
             words.append(chunk)
         w_sb = held.tile([D, M], BF16, name="w_sb")
         nc.sync.dma_start(w_sb[:], w)
         pe_f32 = held.tile([D, N], F32, name="pe_f32")
-        nc.scalar.dma_start(pe_f32[:], pe)
-        offsets = held.tile([P, N // 16], U16, name="offsets")
-        nc.sync.dma_start(offsets[:], offs)
+        nc.sync.dma_start(pe_f32[:], pe)
         bias = held.tile([P, C], F32, name="bias")
         with nc.allow_non_contiguous_dma(reason="512 biases, four to a partition, 128 apart in HBM"):
-            nc.scalar.dma_start(bias[:], b.rearrange("(c p) o -> p (c o)", p=P))
+            nc.sync.dma_start(bias[:], b.rearrange("(c p) o -> p (c o)", p=P))
 
         window = held.tile([D, V], BF16, name="window")
         for q in range(CHUNKS):
             flipped = flip.tile([D, BLOCKS_PER_CHUNK * P], BF16, name=f"flipped{q}")
             for t in range(BLOCKS_PER_CHUNK):
                 nc.tensor.transpose(flipped[:, t * P : (t + 1) * P], words[q][:, t, :], identity[:])
+            in_order = flipped[:].rearrange("k (t p) -> k p t", t=BLOCKS_PER_CHUNK)
             columns = window[:, q * BLOCKS_PER_CHUNK * P : (q + 1) * BLOCKS_PER_CHUNK * P]
+            columns = columns.rearrange("k (p t) -> k p t", t=BLOCKS_PER_CHUNK)
             if q % 2 == 0:
-                nc.vector.tensor_copy(columns, flipped[:])
+                nc.vector.tensor_copy(columns, in_order)
             else:
-                nc.scalar.copy(columns, flipped[:])
+                nc.scalar.copy(columns, in_order)
 
         for c in range(C):
             nc.tensor.matmul(acc[c][:], w_sb[:, c * P : (c + 1) * P], window[:].indirect(offsets[:]), start=True, stop=False)

@@ -30,44 +30,42 @@ def tile_fullencoder_kernel(tc, table, w, b, pe, offs, out):
         identity = held.tile([P, P], BF16, name="identity")
         make_identity(nc, identity[:])
 
-        offsets = held.tile([P, N // 16], U16, name="offsets")
-        nc.sync.dma_start(offsets[:], offs)
-        table_chunks = table.rearrange("(q p t) k -> p q t k", p=P, t=BLOCKS_PER_CHUNK)
+        pe_f32 = held.tile([D, N], F32, name="pe_f32")
+        nc.scalar.dma_start(pe_f32[:], pe)
+        table_blocks = table.rearrange("(t p) k -> p t k", p=P)
         words = []
         for q in range(CHUNKS):
             chunk = held.tile([P, BLOCKS_PER_CHUNK, D], BF16, name=f"words{q}")
             queue = nc.sync if q % 2 == 0 else nc.scalar
-            queue.dma_start(chunk[:], table_chunks[:, q, :, :])
+            queue.dma_start(chunk[:], table_blocks[:, q * BLOCKS_PER_CHUNK : (q + 1) * BLOCKS_PER_CHUNK, :])
             words.append(chunk)
         w_sb = held.tile([D, M], BF16, name="w_sb")
         nc.sync.dma_start(w_sb[:], w)
-        pe_f32 = held.tile([D, N], F32, name="pe_f32")
-        nc.sync.dma_start(pe_f32[:], pe)
+        offsets = held.tile([P, N // 16], U16, name="offsets")
+        nc.sync.dma_start(offsets[:], offs)
         bias = held.tile([P, C], F32, name="bias")
         with nc.allow_non_contiguous_dma(reason="512 biases, four to a partition, 128 apart in HBM"):
-            nc.sync.dma_start(bias[:], b.rearrange("(c p) o -> p (c o)", p=P))
+            nc.scalar.dma_start(bias[:], b.rearrange("(c p) o -> p (c o)", p=P))
 
         window = held.tile([D, V], BF16, name="window")
         for q in range(CHUNKS):
             flipped = flip.tile([D, BLOCKS_PER_CHUNK * P], BF16, name=f"flipped{q}")
             for t in range(BLOCKS_PER_CHUNK):
                 nc.tensor.transpose(flipped[:, t * P : (t + 1) * P], words[q][:, t, :], identity[:])
-            in_order = flipped[:].rearrange("k (t p) -> k p t", t=BLOCKS_PER_CHUNK)
             columns = window[:, q * BLOCKS_PER_CHUNK * P : (q + 1) * BLOCKS_PER_CHUNK * P]
-            columns = columns.rearrange("k (p t) -> k p t", t=BLOCKS_PER_CHUNK)
             if q % 2 == 0:
-                nc.vector.tensor_copy(columns, in_order)
+                nc.vector.tensor_copy(columns, flipped[:])
             else:
-                nc.scalar.copy(columns, in_order)
-
-        for c in range(C):
-            nc.tensor.matmul(acc[c][:], w_sb[:, c * P : (c + 1) * P], window[:].indirect(offsets[:]), start=True, stop=False)
+                nc.scalar.copy(columns, flipped[:])
 
         pe_bf = held.tile([D, N], BF16, name="pe_bf")
         nc.gpsimd.tensor_copy(pe_bf[:], pe_f32[:])
+        for c in range(C):
+            nc.tensor.matmul(acc[c][:], w_sb[:, c * P : (c + 1) * P], pe_bf[:], start=True, stop=False)
+
         out_rows = out.rearrange("(c p) j -> p c j", p=P)
         for c in range(C):
-            nc.tensor.matmul(acc[c][:], w_sb[:, c * P : (c + 1) * P], pe_bf[:], start=False, stop=True)
+            nc.tensor.matmul(acc[c][:], w_sb[:, c * P : (c + 1) * P], window[:].indirect(offsets[:]), start=False, stop=True)
             result = held.tile([P, N], F32, name=f"result{c}")
             if c % 2 == 0:
                 nc.vector.tensor_scalar(result[:], acc[c][:], bias[:, c : c + 1], None, mybir.AluOpType.add)

@@ -9,6 +9,8 @@ BLOCKS = V // P
 CHUNKS = 4
 BLOCKS_PER_CHUNK = BLOCKS // CHUNKS
 C = M // P
+W_PARTS = 2
+GROUPS_PER_PART = C // W_PARTS
 WARMERS = 6
 
 FLOPS = 2 * (2 * D * M * N)
@@ -31,21 +33,24 @@ def tile_fullencoder_kernel(tc, table, w, b, pe, offs, out):
         make_identity(nc, identity[:])
 
         pe_f32 = held.tile([D, N], F32, name="pe_f32")
-        nc.scalar.dma_start(pe_f32[:], pe)
+        nc.sync.dma_start(pe_f32[:], pe)
         table_blocks = table.rearrange("(t p) k -> p t k", p=P)
         words = []
         for q in range(CHUNKS):
             chunk = held.tile([P, BLOCKS_PER_CHUNK, D], BF16, name=f"words{q}")
-            queue = nc.sync if q % 2 == 0 else nc.scalar
-            queue.dma_start(chunk[:], table_blocks[:, q * BLOCKS_PER_CHUNK : (q + 1) * BLOCKS_PER_CHUNK, :])
+            nc.sync.dma_start(chunk[:], table_blocks[:, q * BLOCKS_PER_CHUNK : (q + 1) * BLOCKS_PER_CHUNK, :])
             words.append(chunk)
-        w_sb = held.tile([D, M], BF16, name="w_sb")
-        nc.sync.dma_start(w_sb[:], w)
+        weights = []
+        for part in range(W_PARTS):
+            w_part = held.tile([D, GROUPS_PER_PART * P], BF16, name=f"w_part{part}")
+            nc.sync.dma_start(w_part[:], w[:, part * GROUPS_PER_PART * P : (part + 1) * GROUPS_PER_PART * P])
+            for g in range(GROUPS_PER_PART):
+                weights.append(w_part[:, g * P : (g + 1) * P])
         offsets = held.tile([P, N // 16], U16, name="offsets")
         nc.sync.dma_start(offsets[:], offs)
         bias = held.tile([P, C], F32, name="bias")
         with nc.allow_non_contiguous_dma(reason="512 biases, four to a partition, 128 apart in HBM"):
-            nc.scalar.dma_start(bias[:], b.rearrange("(c p) o -> p (c o)", p=P))
+            nc.sync.dma_start(bias[:], b.rearrange("(c p) o -> p (c o)", p=P))
 
         window = held.tile([D, V], BF16, name="window")
         for q in range(CHUNKS):
@@ -61,11 +66,11 @@ def tile_fullencoder_kernel(tc, table, w, b, pe, offs, out):
         pe_bf = held.tile([D, N], BF16, name="pe_bf")
         nc.gpsimd.tensor_copy(pe_bf[:], pe_f32[:])
         for c in range(C):
-            nc.tensor.matmul(acc[c][:], w_sb[:, c * P : (c + 1) * P], pe_bf[:], start=True, stop=False)
+            nc.tensor.matmul(acc[c][:], weights[c], pe_bf[:], start=True, stop=False)
 
         out_rows = out.rearrange("(c p) j -> p c j", p=P)
         for c in range(C):
-            nc.tensor.matmul(acc[c][:], w_sb[:, c * P : (c + 1) * P], window[:].indirect(offsets[:]), start=False, stop=True)
+            nc.tensor.matmul(acc[c][:], weights[c], window[:].indirect(offsets[:]), start=False, stop=True)
             result = held.tile([P, N], F32, name=f"result{c}")
             if c % 2 == 0:
                 nc.vector.tensor_scalar(result[:], acc[c][:], bias[:, c : c + 1], None, mybir.AluOpType.add)

@@ -11,6 +11,7 @@ BLOCKS_PER_CHUNK = BLOCKS // CHUNKS
 C = M // P
 W_PARTS = 2
 GROUPS_PER_PART = C // W_PARTS
+SUMS = [(c, 0, N) for c in range(C - 1)] + [(C - 1, 0, N // 2), (C - 1, N // 2, N // 2)]
 WARMERS = 6
 
 FLOPS = 2 * (2 * D * M * N)
@@ -65,18 +66,24 @@ def tile_fullencoder_kernel(tc, table, w, b, pe, offs, out):
 
         pe_bf = held.tile([D, N], BF16, name="pe_bf")
         nc.gpsimd.tensor_copy(pe_bf[:], pe_f32[:])
-        for c in range(C):
-            nc.tensor.matmul(acc[c][:], weights[c], pe_bf[:], start=True, stop=False)
+        acc.append(flip.tile([P, N], F32, name="acc4", tag="flipped0"))
+        for s, (c, first, tokens) in enumerate(SUMS):
+            nc.tensor.matmul(
+                acc[s][:, 0:tokens], weights[c], pe_bf[:, first : first + tokens], start=True, stop=False
+            )
 
         out_rows = out.rearrange("(c p) j -> p c j", p=P)
-        for c in range(C):
-            nc.tensor.matmul(acc[c][:], weights[c], window[:].indirect(offsets[:]), start=False, stop=True)
-            result = held.tile([P, N], F32, name=f"result{c}")
-            if c % 2 == 0:
-                nc.vector.tensor_scalar(result[:], acc[c][:], bias[:, c : c + 1], None, mybir.AluOpType.add)
-                nc.sync.dma_start(out_rows[:, c, :], result[:])
+        for s, (c, first, tokens) in enumerate(SUMS):
+            looked_up = window[:].indirect(offsets[:, first // 16 : (first + tokens) // 16])
+            nc.tensor.matmul(acc[s][:, 0:tokens], weights[c], looked_up, start=False, stop=True)
+            result = held.tile([P, tokens], F32, name=f"result{s}")
+            if s % 2 == 0:
+                nc.vector.tensor_scalar(
+                    result[:], acc[s][:, 0:tokens], bias[:, c : c + 1], None, mybir.AluOpType.add
+                )
+                nc.sync.dma_start(out_rows[:, c, first : first + tokens], result[:])
             else:
                 nc.scalar.activation(
-                    result[:], acc[c][:], mybir.ActivationFunctionType.Identity, bias=bias[:, c : c + 1]
+                    result[:], acc[s][:, 0:tokens], mybir.ActivationFunctionType.Identity, bias=bias[:, c : c + 1]
                 )
-                nc.scalar.dma_start(out_rows[:, c, :], result[:])
+                nc.scalar.dma_start(out_rows[:, c, first : first + tokens], result[:])

@@ -86,4 +86,4 @@ def tile_fullencoder_kernel(tc, table, w, b, pe, offs, out):
                 nc.scalar.activation(
                     result[:], acc[s][:, 0:tokens], mybir.ActivationFunctionType.Identity, bias=bias[:, c : c + 1]
                 )
-                nc.scalar.dma_start(out_rows[:, c, first : first + tokens], result[:])
+                nc.sync.dma_start(out_rows[:, c, first : first + tokens], result[:])

@@ -9,8 +9,6 @@ BLOCKS = V // P
 CHUNKS = 4
 BLOCKS_PER_CHUNK = BLOCKS // CHUNKS
 C = M // P
-W_PARTS = 2
-GROUPS_PER_PART = C // W_PARTS
 SUMS = [(c, 0, N) for c in range(C - 1)] + [(C - 1, 0, N // 2), (C - 1, N // 2, N // 2)]
 WARMERS = 6
 
@@ -33,20 +31,17 @@ def tile_fullencoder_kernel(tc, table, w, b, pe, offs, out):
         identity = held.tile([P, P], BF16, name="identity")
         make_identity(nc, identity[:])
 
-        pe_f32 = held.tile([D, N], F32, name="pe_f32")
-        nc.sync.dma_start(pe_f32[:], pe)
-        table_blocks = table.rearrange("(t p) k -> p t k", p=P)
+        table_chunks = table.rearrange("(q p t) k -> q p t k", p=P, t=BLOCKS_PER_CHUNK)
         words = []
         for q in range(CHUNKS):
             chunk = held.tile([P, BLOCKS_PER_CHUNK, D], BF16, name=f"words{q}")
-            nc.sync.dma_start(chunk[:], table_blocks[:, q * BLOCKS_PER_CHUNK : (q + 1) * BLOCKS_PER_CHUNK, :])
+            nc.sync.dma_start(chunk[:], table_chunks[q])
             words.append(chunk)
-        weights = []
-        for part in range(W_PARTS):
-            w_part = held.tile([D, GROUPS_PER_PART * P], BF16, name=f"w_part{part}")
-            nc.sync.dma_start(w_part[:], w[:, part * GROUPS_PER_PART * P : (part + 1) * GROUPS_PER_PART * P])
-            for g in range(GROUPS_PER_PART):
-                weights.append(w_part[:, g * P : (g + 1) * P])
+        pe_f32 = held.tile([D, N], F32, name="pe_f32")
+        nc.sync.dma_start(pe_f32[:], pe)
+        w_tile = held.tile([D, M], BF16, name="w_tile")
+        nc.sync.dma_start(w_tile[:], w)
+        weights = [w_tile[:, c * P : (c + 1) * P] for c in range(C)]
         offsets = held.tile([P, N // 16], U16, name="offsets")
         nc.sync.dma_start(offsets[:], offs)
         bias = held.tile([P, C], F32, name="bias")
@@ -58,14 +53,16 @@ def tile_fullencoder_kernel(tc, table, w, b, pe, offs, out):
             flipped = flip.tile([D, BLOCKS_PER_CHUNK * P], BF16, name=f"flipped{q}")
             for t in range(BLOCKS_PER_CHUNK):
                 nc.tensor.transpose(flipped[:, t * P : (t + 1) * P], words[q][:, t, :], identity[:])
+            in_word_order = flipped[:].rearrange("k (t p) -> k p t", p=P)
             columns = window[:, q * BLOCKS_PER_CHUNK * P : (q + 1) * BLOCKS_PER_CHUNK * P]
+            columns = columns.rearrange("k (p t) -> k p t", t=BLOCKS_PER_CHUNK)
             if q % 2 == 0:
-                nc.vector.tensor_copy(columns, flipped[:])
+                nc.vector.tensor_copy(columns, in_word_order)
             else:
-                nc.scalar.copy(columns, flipped[:])
+                nc.scalar.copy(columns, in_word_order)
 
-        pe_bf = held.tile([D, N], BF16, name="pe_bf")
-        nc.gpsimd.tensor_copy(pe_bf[:], pe_f32[:])
+        pe_bf = held.tile([D, N], BF16, name="pe_bf", tag="words0")
+        nc.vector.tensor_copy(pe_bf[:], pe_f32[:])
         acc.append(flip.tile([P, N], F32, name="acc4", tag="flipped0"))
         for s, (c, first, tokens) in enumerate(SUMS):
             nc.tensor.matmul(

@@ -9,6 +9,8 @@ BLOCKS = V // P
 CHUNKS = 4
 BLOCKS_PER_CHUNK = BLOCKS // CHUNKS
 C = M // P
+W_PARTS = 2
+GROUPS_PER_PART = C // W_PARTS
 SUMS = [(c, 0, N) for c in range(C - 1)] + [(C - 1, 0, N // 2), (C - 1, N // 2, N // 2)]
 WARMERS = 6
 
@@ -37,11 +39,15 @@ def tile_fullencoder_kernel(tc, table, w, b, pe, offs, out):
             chunk = held.tile([P, BLOCKS_PER_CHUNK, D], BF16, name=f"words{q}")
             nc.sync.dma_start(chunk[:], table_chunks[q])
             words.append(chunk)
-        pe_f32 = held.tile([D, N], F32, name="pe_f32")
-        nc.sync.dma_start(pe_f32[:], pe)
-        w_tile = held.tile([D, M], BF16, name="w_tile")
-        nc.sync.dma_start(w_tile[:], w)
-        weights = [w_tile[:, c * P : (c + 1) * P] for c in range(C)]
+            if q == CHUNKS // 2 - 1:
+                pe_f32 = held.tile([D, N], F32, name="pe_f32")
+                nc.sync.dma_start(pe_f32[:], pe)
+        weights = []
+        for part in range(W_PARTS):
+            w_part = held.tile([D, GROUPS_PER_PART * P], BF16, name=f"w_part{part}")
+            nc.sync.dma_start(w_part[:], w[:, part * GROUPS_PER_PART * P : (part + 1) * GROUPS_PER_PART * P])
+            for g in range(GROUPS_PER_PART):
+                weights.append(w_part[:, g * P : (g + 1) * P])
         offsets = held.tile([P, N // 16], U16, name="offsets")
         nc.sync.dma_start(offsets[:], offs)
         bias = held.tile([P, C], F32, name="bias")

@@ -5,9 +5,7 @@ BF16, F32, U16 = mybir.dt.bfloat16, mybir.dt.float32, mybir.dt.uint16
 
 P = 128
 V, D, M, N = 1024, 128, 512, 256
-BLOCKS = V // P
-CHUNKS = 4
-BLOCKS_PER_CHUNK = BLOCKS // CHUNKS
+CHUNKS = [2, 3, 2, 1]
 C = M // P
 W_PARTS = 2
 GROUPS_PER_PART = C // W_PARTS
@@ -33,13 +31,15 @@ def tile_fullencoder_kernel(tc, table, w, b, pe, offs, out):
         identity = held.tile([P, P], BF16, name="identity")
         make_identity(nc, identity[:])
 
-        table_chunks = table.rearrange("(q p t) k -> q p t k", p=P, t=BLOCKS_PER_CHUNK)
         words = []
-        for q in range(CHUNKS):
-            chunk = held.tile([P, BLOCKS_PER_CHUNK, D], BF16, name=f"words{q}")
-            nc.sync.dma_start(chunk[:], table_chunks[q])
+        first_word = 0
+        for q, blocks in enumerate(CHUNKS):
+            chunk = held.tile([P, blocks, D], BF16, name=f"words{q}")
+            rows = table[first_word : first_word + blocks * P, :]
+            nc.sync.dma_start(chunk[:], rows.rearrange("(p t) k -> p t k", p=P))
             words.append(chunk)
-            if q == CHUNKS // 2 - 1:
+            first_word += blocks * P
+            if q == 1:
                 pe_f32 = held.tile([D, N], F32, name="pe_f32")
                 nc.sync.dma_start(pe_f32[:], pe)
         weights = []
@@ -55,17 +55,18 @@ def tile_fullencoder_kernel(tc, table, w, b, pe, offs, out):
             nc.sync.dma_start(bias[:], b.rearrange("(c p) o -> p (c o)", p=P))
 
         window = held.tile([D, V], BF16, name="window")
-        for q in range(CHUNKS):
-            flipped = flip.tile([D, BLOCKS_PER_CHUNK * P], BF16, name=f"flipped{q}")
-            for t in range(BLOCKS_PER_CHUNK):
+        first_word = 0
+        for q, blocks in enumerate(CHUNKS):
+            flipped = flip.tile([D, blocks * P], BF16, name=f"flipped{q}")
+            for t in range(blocks):
                 nc.tensor.transpose(flipped[:, t * P : (t + 1) * P], words[q][:, t, :], identity[:])
             in_word_order = flipped[:].rearrange("k (t p) -> k p t", p=P)
-            columns = window[:, q * BLOCKS_PER_CHUNK * P : (q + 1) * BLOCKS_PER_CHUNK * P]
-            columns = columns.rearrange("k (p t) -> k p t", t=BLOCKS_PER_CHUNK)
+            columns = window[:, first_word : first_word + blocks * P].rearrange("k (p t) -> k p t", t=blocks)
             if q % 2 == 0:
                 nc.vector.tensor_copy(columns, in_word_order)
             else:
                 nc.scalar.copy(columns, in_word_order)
+            first_word += blocks * P
 
         pe_bf = held.tile([D, N], BF16, name="pe_bf", tag="words0")
         nc.vector.tensor_copy(pe_bf[:], pe_f32[:])

import concourse.mybir as mybir
from concourse.masks import make_identity

BF16, F32, U16 = mybir.dt.bfloat16, mybir.dt.float32, mybir.dt.uint16

P = 128
V, D, M, N = 1024, 128, 512, 256
CHUNKS = [2, 3, 2, 1]
C = M // P
W_PARTS = 2
GROUPS_PER_PART = C // W_PARTS
SUMS = [(c, 0, N) for c in range(C - 1)] + [(C - 1, 0, N // 2), (C - 1, N // 2, N // 2)]
WARMERS = 6

FLOPS = 2 * (2 * D * M * N)


def tile_fullencoder_kernel(tc, table, w, b, pe, offs, out):
    nc = tc.nc
    with (
        tc.tile_pool(name="held", bufs=1) as held,
        tc.psum_pool(name="flip", bufs=1) as flip,
        tc.psum_pool(name="sums", bufs=1) as sums,
    ):
        zeros = held.tile([P, N], BF16, name="zeros")
        nc.gpsimd.memset(zeros[:], 0.0)
        acc = [sums.tile([P, N], F32, name=f"acc{c}") for c in range(C)]
        for warmer in range(WARMERS):
            nc.tensor.matmul(acc[warmer % C][:], zeros[:, 0:P], zeros[:], start=True, stop=True)

        identity = held.tile([P, P], BF16, name="identity")
        make_identity(nc, identity[:])

        words = []
        first_word = 0
        for q, blocks in enumerate(CHUNKS):
            chunk = held.tile([P, blocks, D], BF16, name=f"words{q}")
            rows = table[first_word : first_word + blocks * P, :]
            nc.sync.dma_start(chunk[:], rows.rearrange("(p t) k -> p t k", p=P))
            words.append(chunk)
            first_word += blocks * P
            if q == 1:
                pe_f32 = held.tile([D, N], F32, name="pe_f32")
                nc.sync.dma_start(pe_f32[:], pe)
        weights = []
        for part in range(W_PARTS):
            w_part = held.tile([D, GROUPS_PER_PART * P], BF16, name=f"w_part{part}")
            nc.sync.dma_start(w_part[:], w[:, part * GROUPS_PER_PART * P : (part + 1) * GROUPS_PER_PART * P])
            for g in range(GROUPS_PER_PART):
                weights.append(w_part[:, g * P : (g + 1) * P])
        offsets = held.tile([P, N // 16], U16, name="offsets")
        nc.sync.dma_start(offsets[:], offs)
        bias = held.tile([P, C], F32, name="bias")
        with nc.allow_non_contiguous_dma(reason="512 biases, four to a partition, 128 apart in HBM"):
            nc.sync.dma_start(bias[:], b.rearrange("(c p) o -> p (c o)", p=P))

        window = held.tile([D, V], BF16, name="window")
        first_word = 0
        for q, blocks in enumerate(CHUNKS):
            flipped = flip.tile([D, blocks * P], BF16, name=f"flipped{q}")
            for t in range(blocks):
                nc.tensor.transpose(flipped[:, t * P : (t + 1) * P], words[q][:, t, :], identity[:])
            in_word_order = flipped[:].rearrange("k (t p) -> k p t", p=P)
            columns = window[:, first_word : first_word + blocks * P].rearrange("k (p t) -> k p t", t=blocks)
            if q % 2 == 0:
                nc.vector.tensor_copy(columns, in_word_order)
            else:
                nc.scalar.copy(columns, in_word_order)
            first_word += blocks * P

        pe_bf = held.tile([D, N], BF16, name="pe_bf", tag="words0")
        nc.vector.tensor_copy(pe_bf[:], pe_f32[:])
        acc.append(flip.tile([P, N], F32, name="acc4", tag="flipped0"))
        for s, (c, first, tokens) in enumerate(SUMS):
            nc.tensor.matmul(
                acc[s][:, 0:tokens], weights[c], pe_bf[:, first : first + tokens], start=True, stop=False
            )

        out_rows = out.rearrange("(c p) j -> p c j", p=P)
        for s, (c, first, tokens) in enumerate(SUMS):
            looked_up = window[:].indirect(offsets[:, first // 16 : (first + tokens) // 16])
            nc.tensor.matmul(acc[s][:, 0:tokens], weights[c], looked_up, start=False, stop=True)
            result = held.tile([P, tokens], F32, name=f"result{s}")
            if s % 2 == 0:
                nc.vector.tensor_scalar(
                    result[:], acc[s][:, 0:tokens], bias[:, c : c + 1], None, mybir.AluOpType.add
                )
                nc.sync.dma_start(out_rows[:, c, first : first + tokens], result[:])
            else:
                nc.scalar.activation(
                    result[:], acc[s][:, 0:tokens], mybir.ActivationFunctionType.Identity, bias=bias[:, c : c + 1]
                )
                nc.sync.dma_start(out_rows[:, c, first : first + tokens], result[:])
